import numpy as np
import ml_dtypes


def mxq(x, axis, fmt="e4m3"):
    dtype, down = {"e4m3": (ml_dtypes.float8_e4m3fn, 7), "e5m2": (ml_dtypes.float8_e5m2, 14)}[fmt]
    v = np.moveaxis(np.asarray(x, np.float32).astype(ml_dtypes.bfloat16).astype(np.float64), axis, -1)
    blocks = v.reshape(v.shape[:-1] + (-1, 32))
    amax = np.abs(blocks).max(-1, keepdims=True)
    byte = np.maximum(np.where(amax > 0, np.frexp(amax)[1] - 1 + 127, 0) - down, 1)
    scale = np.exp2(byte - 127.0)
    codes = (blocks / scale).astype(np.float32).astype(dtype).astype(np.float64)
    return np.moveaxis((codes * scale).reshape(v.shape), -1, axis)


WIDE = False


def mx_kscale(k):
    if not WIDE:
        return np.ones(k)
    levels = np.array([10, -10, 5, -5, 0])
    a = np.random.permutation(np.resize(levels, k // 512 * 4)).reshape(k // 512, 4)
    idx = np.arange(k)
    return np.exp2(a[idx // 512, idx % 128 // 32])


BF16 = ml_dtypes.bfloat16


def bf(x):
    return np.asarray(x, np.float32).astype(BF16)


def f64(x):
    return np.asarray(x).astype(np.float64)


B, S, D, F = 2, 256, 1024, 3072


def silu(v):
    return v / (1.0 + np.exp(-v))


def setup_inputs():
    s, t = mx_kscale(D), mx_kscale(F)
    return {"x": bf(np.random.standard_normal((B, S, D)) * s),
            "weight1": bf(np.random.standard_normal((F, D)) * 0.03 / s[None, :]),
            "weight2": bf(np.random.standard_normal((F, D)) * 0.03 / s[None, :] * t[:, None]),
            "weight3": bf(np.random.standard_normal((D, F)) * 0.03 / t[None, :])}


def reference(x, weight1, weight2, weight3):
    xq = mxq(f64(x), 2, "e4m3")
    a = np.einsum('bsd,fd->bsf', xq, mxq(f64(weight1), 1, "e4m3"))
    b = np.einsum('bsd,fd->bsf', xq, mxq(f64(weight2), 1, "e4m3"))
    h = silu(a) * b
    return np.einsum('bsf,df->bsd', mxq(h, 2, "e4m3"), mxq(f64(weight3), 1, "e4m3"))

@@ -1,0 +1,247 @@
+from contextlib import ExitStack
+
+import concourse.mybir as mybir
+from concourse.masks import make_identity
+
+F32 = mybir.dt.float32
+BF16 = mybir.dt.bfloat16
+U32 = mybir.dt.uint32
+U8 = mybir.dt.uint8
+FP8X4 = mybir.dt.float8_e4m3fn_x4
+SILU = mybir.ActivationFunctionType.Silu
+MULT = mybir.AluOpType.mult
+
+P = 128
+TOK = 512
+D = 1024
+F = 3072
+FLOPS = 2 * TOK * D * F * 3
+
+N_WIN = F // 256
+N_W3 = 6
+N_CHUNK = N_WIN + N_W3
+RAW_BUFS = 14
+
+
+def tile_nf4mlp_kernel(tc, x, weight1, weight2, weight3, out):
+    nc = tc.nc
+    xf = x.flatten_outer_dims()
+    of = out.flatten_outer_dims()
+    w1v = weight1.rearrange("(v r e) k -> v r (e k)", r=P, e=2)
+    w2v = weight2.rearrange("(v r e) k -> v r (e k)", r=P, e=2)
+    w3v = weight3.rearrange("(h j p) (b c) -> h b p j c", j=4, p=P, c=1024)
+
+    with ExitStack() as ctx:
+        keep = ctx.enter_context(tc.tile_pool(name="keep", bufs=1))
+        xrp = ctx.enter_context(tc.tile_pool(name="xrp", bufs=4))
+        rawp = ctx.enter_context(tc.tile_pool(name="rawp", bufs=RAW_BUFS))
+        gp = ctx.enter_context(tc.tile_pool(name="gp", bufs=3))
+        cp = ctx.enter_context(tc.tile_pool(name="cp", bufs=3))
+        sp = ctx.enter_context(tc.tile_pool(name="sp", bufs=4))
+        hpp = ctx.enter_context(tc.tile_pool(name="hpp", bufs=2))
+        hgp = ctx.enter_context(tc.tile_pool(name="hgp", bufs=2))
+        op = ctx.enter_context(tc.tile_pool(name="op", bufs=4))
+        tp = ctx.enter_context(tc.psum_pool(name="tp", bufs=4))
+        accp = ctx.enter_context(tc.psum_pool(name="accp", bufs=4))
+        ctx.enter_context(tc.manual_schedule())
+
+        ident = keep.tile([P, P], F32)
+        make_identity(nc, ident[:])
+        warm_in = keep.tile([P, 1], F32)
+        warm_out = keep.tile([P, 1], F32)
+        nc.vector.memset(warm_in[:], 0.0)
+        nc.scalar.activation(out=warm_out[:], in_=warm_in[:], func=SILU)
+
+        xc = keep.tile([P, 1024], U32, align_bytes=64)
+        xs = keep.tile([P, 1024], U8, align_bytes=64)
+        hc = keep.tile([P, 6, 512], U32, align_bytes=64)
+        hs = keep.tile([P, 6, 512], U8, align_bytes=64)
+
+        xr32 = []
+        for i in range(4):
+            xr = xrp.tile([P, D], BF16, tag="xr")
+            nc.sync.dma_start(out=xr[:], in_=xf[P * i : P * i + P, :])
+            xr32.append(xr[:].bitcast(F32))
+
+        raw32 = {}
+
+        def load_chunk(c):
+            raw = rawp.tile([P, 4096], BF16, tag="raw")
+            if c < N_WIN:
+                nc.sync.dma_start(out=raw[:, 0:2048], in_=w1v[c])
+                nc.sync.dma_start(out=raw[:, 2048:4096], in_=w2v[c])
+            else:
+                b = c - N_WIN
+                nc.sync.dma_start(
+                    out=raw[:].rearrange("p (j c) -> p j c", j=4),
+                    in_=w3v[b // 3, b % 3],
+                )
+            raw32[c] = raw[:].bitcast(F32)
+
+        for c in range(RAW_BUFS):
+            load_chunk(c)
+
+        def transpose_bunch(src, vector_banks):
+            g = gp.tile([P, 4096], BF16, tag="g", align_bytes=64)
+            g32 = g[:].bitcast(F32)
+            banks = []
+            for bank in range(4):
+                xt = tp.tile([P, 2, 256], F32, tag="xt")
+                for c in range(2):
+                    for u in range(2):
+                        nc.tensor.transpose(
+                            xt[:, u, P * c : P * c + P], src(bank, u, c), ident[:]
+                        )
+                banks.append(xt)
+            for bank in range(4):
+                dst = g32[:, 512 * bank : 512 * bank + 512].rearrange(
+                    "p (r u) -> p r u", u=2
+                )
+                srcv = banks[bank][:].rearrange("p u r -> p r u")
+                if bank in vector_banks:
+                    nc.vector.tensor_copy(out=dst, in_=srcv)
+                else:
+                    nc.scalar.copy(out=dst, in_=srcv)
+            return g
+
+        def quantise(g, codes, scales):
+            for h in range(2):
+                nc.vector.quantize_mx(
+                    out=codes[:, 512 * h : 512 * h + 512].bitcast(FP8X4),
+                    scales=scales[:, 512 * h : 512 * h + 512],
+                    in_=g[:, 2048 * h : 2048 * h + 2048],
+                )
+
+        def x_src(bank, u, c):
+            off = (bank // 2) * 256 + u * P
+            return xr32[2 * (bank % 2) + c][:, off : off + P]
+
+        def w_src(v):
+            def src(bank, u, c):
+                off = (bank // 2) * 1024 + c * 512 + (bank % 2) * 256 + u * P
+                return raw32[v][:, off : off + P]
+
+            return src
+
+        def w3_src(b):
+            def src(bank, u, c):
+                off = (2 * (bank % 2) + c) * 512 + (bank // 2) * 256 + u * P
+                return raw32[N_WIN + b][:, off : off + P]
+
+            return src
+
+        def new_codes():
+            codes = cp.tile([P, 1024], U32, tag="codes", align_bytes=64)
+            scales = cp.tile([P, 1024], U8, tag="scales", align_bytes=64)
+            return codes, scales
+
+        def gate_up(codes, scales):
+            accs = []
+            for e in range(2):
+                for w in range(2):
+                    acc = accp.tile([P, 512], F32, tag="acc")
+                    for gk in range(2):
+                        col = (2 * w + gk) * 256 + P * e
+                        nc.tensor.matmul_mx(
+                            out=acc[:],
+                            lhsT=codes[:, col : col + P].bitcast(FP8X4),
+                            lhsT_scale=scales[:, col : col + P],
+                            rhs=xc[:, 512 * gk : 512 * gk + 512].bitcast(FP8X4),
+                            rhs_scale=xs[:, 512 * gk : 512 * gk + 512],
+                            start=(gk == 0),
+                            stop=(gk == 1),
+                        )
+                    accs.append(acc)
+            return accs
+
+        def quantise_h(hg, g):
+            nc.vector.quantize_mx(
+                out=hc[:, g, :].bitcast(FP8X4),
+                scales=hs[:, g, :],
+                in_=hg[:].rearrange("p w t -> p (w t)"),
+            )
+
+        gx = transpose_bunch(x_src, (1, 3))
+        quantise(gx, xc, xs)
+        g0 = transpose_bunch(w_src(0), (1, 3))
+        cur = new_codes()
+        quantise(g0, cur[0], cur[1])
+
+        hp = None
+        pending = None
+        for v in range(N_WIN):
+            if v + 1 < N_WIN:
+                gn = transpose_bunch(w_src(v + 1), (1, 3) if v == 0 else ())
+            else:
+                gn = transpose_bunch(w3_src(0), ())
+            if v + RAW_BUFS < N_CHUNK:
+                load_chunk(v + RAW_BUFS)
+            accs = gate_up(cur[0], cur[1])
+            ss = []
+            for e in range(2):
+                s = sp.tile([P, 512], F32, tag="s")
+                nc.scalar.activation(out=s[:], in_=accs[2 * e][:], func=SILU)
+                ss.append(s)
+            cur = new_codes()
+            quantise(gn, cur[0], cur[1])
+            if pending is not None:
+                quantise_h(pending[0], pending[1])
+                pending = None
+            if v % 2 == 0:
+                hp = hpp.tile([P, 4, 512], BF16, tag="hp")
+            for e in range(2):
+                nc.vector.tensor_tensor(
+                    out=hp[:, 2 * (v % 2) + e, :],
+                    in0=ss[e][:],
+                    in1=accs[2 * e + 1][:],
+                    op=MULT,
+                )
+            if v % 2 == 1:
+                hg = hgp.tile([P, 512, 4], BF16, tag="hg", align_bytes=64)
+                nc.vector.tensor_copy(
+                    out=hg[:].rearrange("p (c i) t -> p c t i", i=4),
+                    in_=hp[:].rearrange("p t (c i) -> p c t i", i=4),
+                )
+                pending = (hg, v // 2)
+
+        acc2 = None
+        for b in range(N_W3):
+            half, gpair = b // 3, b % 3
+            nxt = None
+            if b + 1 < N_W3:
+                gn = transpose_bunch(w3_src(b + 1), (1, 3))
+            if gpair == 0:
+                acc2 = []
+                for i in range(4):
+                    acc = accp.tile([P, 512], F32, tag="acc")
+                    acc2.append(acc)
+            if pending is not None:
+                quantise_h(pending[0], pending[1])
+                pending = None
+            for i in range(4):
+                for gl in range(2):
+                    g = 2 * gpair + gl
+                    nc.tensor.matmul_mx(
+                        out=acc2[i][:],
+                        lhsT=hc[:, g, P * i : P * i + P].bitcast(FP8X4),
+                        lhsT_scale=hs[:, g, P * i : P * i + P],
+                        rhs=cur[0][:, 512 * gl : 512 * gl + 512].bitcast(FP8X4),
+                        rhs_scale=cur[1][:, 512 * gl : 512 * gl + 512],
+                        start=(g == 0),
+                        stop=(g == 5),
+                    )
+            if b + 1 < N_W3:
+                nxt = new_codes()
+                quantise(gn, nxt[0], nxt[1])
+                cur = nxt
+            if gpair == 2:
+                for i in range(4):
+                    o = op.tile([P, 512], F32, tag="o")
+                    if i % 2 == 0:
+                        nc.scalar.copy(out=o[:], in_=acc2[i][:])
+                    else:
+                        nc.vector.tensor_copy(out=o[:], in_=acc2[i][:])
+                    nc.sync.dma_start(
+                        out=of[P * i : P * i + P, 512 * half : 512 * half + 512],
+                        in_=o[:],
+                    )

@@ -21,6 +21,7 @@ N_WIN = F // 256
 N_W3 = 6
 N_CHUNK = N_WIN + N_W3
 RAW_BUFS = 14
+WARM = 10
 
 
 def tile_nf4mlp_kernel(tc, x, weight1, weight2, weight3, out):
@@ -41,10 +42,13 @@ def tile_nf4mlp_kernel(tc, x, weight1, weight2, weight3, out):
         hpp = ctx.enter_context(tc.tile_pool(name="hpp", bufs=2))
         hgp = ctx.enter_context(tc.tile_pool(name="hgp", bufs=2))
         op = ctx.enter_context(tc.tile_pool(name="op", bufs=4))
+        olp = ctx.enter_context(tc.tile_pool(name="olp", bufs=2))
         tp = ctx.enter_context(tc.psum_pool(name="tp", bufs=4))
         accp = ctx.enter_context(tc.psum_pool(name="accp", bufs=4))
         ctx.enter_context(tc.manual_schedule())
 
+        zeros = keep.tile([P, 512], BF16)
+        nc.vector.memset(zeros[:], 0.0)
         ident = keep.tile([P, P], F32)
         make_identity(nc, ident[:])
         warm_in = keep.tile([P, 1], F32)
@@ -81,7 +85,15 @@ def tile_nf4mlp_kernel(tc, x, weight1, weight2, weight3, out):
         for c in range(RAW_BUFS):
             load_chunk(c)
 
-        def transpose_bunch(src, vector_banks):
+        idle = accp.tile([P, 512], F32, tag="acc")
+
+        def keep_clock(n):
+            for k in range(n):
+                nc.tensor.matmul(
+                    out=idle[:], lhsT=zeros[:, 0:P], rhs=zeros[:], start=True, stop=True
+                )
+
+        def transpose_bunch(src, vector_banks, block_of=None, fill=0):
             g = gp.tile([P, 4096], BF16, tag="g", align_bytes=64)
             g32 = g[:].bitcast(F32)
             banks = []
@@ -93,8 +105,11 @@ def tile_nf4mlp_kernel(tc, x, weight1, weight2, weight3, out):
                             xt[:, u, P * c : P * c + P], src(bank, u, c), ident[:]
                         )
                 banks.append(xt)
+                if bank % 2 == 1:
+                    keep_clock(fill)
             for bank in range(4):
-                dst = g32[:, 512 * bank : 512 * bank + 512].rearrange(
+                blk = bank if block_of is None else block_of[bank]
+                dst = g32[:, 512 * blk : 512 * blk + 512].rearrange(
                     "p (r u) -> p r u", u=2
                 )
                 srcv = banks[bank][:].rearrange("p u r -> p r u")
@@ -104,17 +119,18 @@ def tile_nf4mlp_kernel(tc, x, weight1, weight2, weight3, out):
                     nc.scalar.copy(out=dst, in_=srcv)
             return g
 
-        def quantise(g, codes, scales):
-            for h in range(2):
+        def quantise(g, codes, scales, pieces=2):
+            w = 1024 // pieces
+            for h in range(pieces):
                 nc.vector.quantize_mx(
-                    out=codes[:, 512 * h : 512 * h + 512].bitcast(FP8X4),
-                    scales=scales[:, 512 * h : 512 * h + 512],
-                    in_=g[:, 2048 * h : 2048 * h + 2048],
+                    out=codes[:, w * h : w * h + w].bitcast(FP8X4),
+                    scales=scales[:, w * h : w * h + w],
+                    in_=g[:, 4 * w * h : 4 * w * h + 4 * w],
                 )
 
         def x_src(bank, u, c):
-            off = (bank // 2) * 256 + u * P
-            return xr32[2 * (bank % 2) + c][:, off : off + P]
+            off = (bank % 2) * 256 + u * P
+            return xr32[2 * (bank // 2) + c][:, off : off + P]
 
         def w_src(v):
             def src(bank, u, c):
@@ -135,24 +151,46 @@ def tile_nf4mlp_kernel(tc, x, weight1, weight2, weight3, out):
             scales = cp.tile([P, 1024], U8, tag="scales", align_bytes=64)
             return codes, scales
 
-        def gate_up(codes, scales):
-            accs = []
+        def gate_up_pass(acc, cs, e, w, gk):
+            col = (2 * w + gk) * 256 + P * e
+            nc.tensor.matmul_mx(
+                out=acc[:],
+                lhsT=cs[0][:, col : col + P].bitcast(FP8X4),
+                lhsT_scale=cs[1][:, col : col + P],
+                rhs=xc[:, 512 * gk : 512 * gk + 512].bitcast(FP8X4),
+                rhs_scale=xs[:, 512 * gk : 512 * gk + 512],
+                start=(gk == 0),
+                stop=(gk == 1),
+            )
+
+        def gate_up(cs):
+            accs = {}
             for e in range(2):
                 for w in range(2):
                     acc = accp.tile([P, 512], F32, tag="acc")
                     for gk in range(2):
-                        col = (2 * w + gk) * 256 + P * e
-                        nc.tensor.matmul_mx(
-                            out=acc[:],
-                            lhsT=codes[:, col : col + P].bitcast(FP8X4),
-                            lhsT_scale=scales[:, col : col + P],
-                            rhs=xc[:, 512 * gk : 512 * gk + 512].bitcast(FP8X4),
-                            rhs_scale=xs[:, 512 * gk : 512 * gk + 512],
-                            start=(gk == 0),
-                            stop=(gk == 1),
-                        )
-                    accs.append(acc)
+                        gate_up_pass(acc, cs, e, w, gk)
+                    accs[(e, w)] = acc
             return accs
+
+        def gate_up_first(cs):
+            accs = {}
+            for w in range(2):
+                for e in range(2):
+                    acc = accp.tile([P, 512], F32, tag="acc")
+                    accs[(e, w)] = acc
+                for gk in range(2):
+                    for e in range(2):
+                        gate_up_pass(accs[(e, w)], cs, e, w, gk)
+            return accs
+
+        def silu(accs):
+            ss = []
+            for e in range(2):
+                s = sp.tile([P, 512], F32, tag="s")
+                nc.scalar.activation(out=s[:], in_=accs[(e, 0)][:], func=SILU)
+                ss.append(s)
+            return ss
 
         def quantise_h(hg, g):
             nc.vector.quantize_mx(
@@ -161,39 +199,23 @@ def tile_nf4mlp_kernel(tc, x, weight1, weight2, weight3, out):
                 in_=hg[:].rearrange("p w t -> p (w t)"),
             )
 
-        gx = transpose_bunch(x_src, (1, 3))
-        quantise(gx, xc, xs)
-        g0 = transpose_bunch(w_src(0), (1, 3))
-        cur = new_codes()
-        quantise(g0, cur[0], cur[1])
+        state = {"hp": None, "pending": None}
 
-        hp = None
-        pending = None
-        for v in range(N_WIN):
-            if v + 1 < N_WIN:
-                gn = transpose_bunch(w_src(v + 1), (1, 3) if v == 0 else ())
-            else:
-                gn = transpose_bunch(w3_src(0), ())
-            if v + RAW_BUFS < N_CHUNK:
-                load_chunk(v + RAW_BUFS)
-            accs = gate_up(cur[0], cur[1])
-            ss = []
-            for e in range(2):
-                s = sp.tile([P, 512], F32, tag="s")
-                nc.scalar.activation(out=s[:], in_=accs[2 * e][:], func=SILU)
-                ss.append(s)
-            cur = new_codes()
-            quantise(gn, cur[0], cur[1])
-            if pending is not None:
-                quantise_h(pending[0], pending[1])
-                pending = None
+        def flush_pending():
+            if state["pending"] is not None:
+                quantise_h(state["pending"][0], state["pending"][1])
+                state["pending"] = None
+
+        def gate(v, ss, accs):
             if v % 2 == 0:
                 hp = hpp.tile([P, 4, 512], BF16, tag="hp")
+                state["hp"] = hp
+            hp = state["hp"]
             for e in range(2):
                 nc.vector.tensor_tensor(
                     out=hp[:, 2 * (v % 2) + e, :],
                     in0=ss[e][:],
-                    in1=accs[2 * e + 1][:],
+                    in1=accs[(e, 1)][:],
                     op=MULT,
                 )
             if v % 2 == 1:
@@ -202,46 +224,89 @@ def tile_nf4mlp_kernel(tc, x, weight1, weight2, weight3, out):
                     out=hg[:].rearrange("p (c i) t -> p c t i", i=4),
                     in_=hp[:].rearrange("p t (c i) -> p c t i", i=4),
                 )
-                pending = (hg, v // 2)
+                state["pending"] = (hg, v // 2)
 
+        keep_clock(WARM)
+        gx = transpose_bunch(x_src, (), block_of=(0, 2, 1, 3), fill=1)
+        quantise(gx, xc, xs)
+        g0 = transpose_bunch(w_src(0), (), fill=1)
+        cur = new_codes()
+        quantise(g0, cur[0], cur[1], pieces=4)
+        accs = gate_up_first(cur)
+        gn = transpose_bunch(w_src(1), (1, 3))
+        load_chunk(RAW_BUFS)
+        ss = silu(accs)
+        cur = new_codes()
+        quantise(gn, cur[0], cur[1])
+        gate(0, ss, accs)
+
+        for v in range(1, N_WIN):
+            if v + 1 < N_WIN:
+                gn = transpose_bunch(w_src(v + 1), ())
+            else:
+                gn = transpose_bunch(w3_src(0), ())
+            if v + RAW_BUFS < N_CHUNK:
+                load_chunk(v + RAW_BUFS)
+            accs = gate_up(cur)
+            ss = silu(accs)
+            cur = new_codes()
+            quantise(gn, cur[0], cur[1])
+            flush_pending()
+            gate(v, ss, accs)
+
+        def down_pass(acc, i, g, cs, col, n):
+            nc.tensor.matmul_mx(
+                out=acc,
+                lhsT=hc[:, g, P * i : P * i + P].bitcast(FP8X4),
+                lhsT_scale=hs[:, g, P * i : P * i + P],
+                rhs=cs[0][:, col : col + n].bitcast(FP8X4),
+                rhs_scale=cs[1][:, col : col + n],
+                start=(g == 0),
+                stop=(g == 5),
+            )
+
+        def store(i, acc, half, on_vector):
+            o = op.tile([P, 512], F32, tag="o")
+            if on_vector:
+                nc.vector.tensor_copy(out=o[:], in_=acc[:])
+            else:
+                nc.scalar.copy(out=o[:], in_=acc[:])
+            nc.sync.dma_start(
+                out=of[P * i : P * i + P, 512 * half : 512 * half + 512], in_=o[:]
+            )
+
+        w3codes = {0: cur}
         acc2 = None
         for b in range(N_W3):
             half, gpair = b // 3, b % 3
-            nxt = None
+            n_tok = 4 if half == 0 else 3
             if b + 1 < N_W3:
                 gn = transpose_bunch(w3_src(b + 1), (1, 3))
             if gpair == 0:
                 acc2 = []
-                for i in range(4):
+                for i in range(n_tok):
                     acc = accp.tile([P, 512], F32, tag="acc")
                     acc2.append(acc)
-            if pending is not None:
-                quantise_h(pending[0], pending[1])
-                pending = None
-            for i in range(4):
+            flush_pending()
+            for i in range(n_tok):
                 for gl in range(2):
-                    g = 2 * gpair + gl
-                    nc.tensor.matmul_mx(
-                        out=acc2[i][:],
-                        lhsT=hc[:, g, P * i : P * i + P].bitcast(FP8X4),
-                        lhsT_scale=hs[:, g, P * i : P * i + P],
-                        rhs=cur[0][:, 512 * gl : 512 * gl + 512].bitcast(FP8X4),
-                        rhs_scale=cur[1][:, 512 * gl : 512 * gl + 512],
-                        start=(g == 0),
-                        stop=(g == 5),
-                    )
+                    down_pass(acc2[i][:], i, 2 * gpair + gl, w3codes[b], 512 * gl, 512)
             if b + 1 < N_W3:
-                nxt = new_codes()
-                quantise(gn, nxt[0], nxt[1])
-                cur = nxt
+                w3codes[b + 1] = new_codes()
+                quantise(gn, w3codes[b + 1][0], w3codes[b + 1][1])
             if gpair == 2:
-                for i in range(4):
-                    o = op.tile([P, 512], F32, tag="o")
-                    if i % 2 == 0:
-                        nc.scalar.copy(out=o[:], in_=acc2[i][:])
-                    else:
-                        nc.vector.tensor_copy(out=o[:], in_=acc2[i][:])
-                    nc.sync.dma_start(
-                        out=of[P * i : P * i + P, 512 * half : 512 * half + 512],
-                        in_=o[:],
-                    )
+                for i in range(n_tok):
+                    store(i, acc2[i], half, i % 2 == 1)
+
+        for q in range(2):
+            last = tp.tile([P, 2, 256], F32, tag="xt")
+            for g in range(6):
+                down_pass(last[:, 0, :], 3, g, w3codes[3 + g // 2], 512 * (g % 2) + 256 * q, 256)
+            ol = olp.tile([P, 256], F32, tag="ol")
+            if q == 0:
+                nc.vector.tensor_copy(out=ol[:], in_=last[:, 0, :])
+            else:
+                nc.scalar.copy(out=ol[:], in_=last[:, 0, :])
+            nc.sync.dma_start(
+                out=of[3 * P : 4 * P, 512 + 256 * q : 512 + 256 * q + 256], in_=ol[:]
+            )

@@ -12,301 +12,267 @@ SILU = mybir.ActivationFunctionType.Silu
 MULT = mybir.AluOpType.mult
 
 P = 128
-TOK = 512
-D = 1024
-F = 3072
-FLOPS = 2 * TOK * D * F * 3
+TOKENS = 512
+D_MODEL = 1024
+D_FF = 3072
+FLOPS = 2 * TOKENS * D_MODEL * D_FF * 3
 
-N_WIN = F // 256
-N_W3 = 6
-N_CHUNK = N_WIN + N_W3
-RAW_BUFS = 14
-WARM = 10
+BANK = 512
+T_BANKS = 4
+N_WINDOWS = D_FF // 256
+N_PASSES_2 = D_FF // 512
+N_RUNS = 4
+N_CHUNKS = N_WINDOWS + 6
+RAW_CHUNKS = 12
 
 
 def tile_nf4mlp_kernel(tc, x, weight1, weight2, weight3, out):
     nc = tc.nc
-    xf = x.flatten_outer_dims()
-    of = out.flatten_outer_dims()
-    w1v = weight1.rearrange("(v r e) k -> v r (e k)", r=P, e=2)
-    w2v = weight2.rearrange("(v r e) k -> v r (e k)", r=P, e=2)
-    w3v = weight3.rearrange("(h j p) (b c) -> h b p j c", j=4, p=P, c=1024)
+    x_rows = x.flatten_outer_dims()
+    out_rows = out.flatten_outer_dims()
+    w1_windows = weight1.rearrange("(v r e) k -> v r (e k)", r=P, e=2)
+    w2_windows = weight2.rearrange("(v r e) k -> v r (e k)", r=P, e=2)
+    w3_chunks = weight3.rearrange("(half j p) (b c) -> half b p j c", j=4, p=P, c=1024)
 
     with ExitStack() as ctx:
         keep = ctx.enter_context(tc.tile_pool(name="keep", bufs=1))
-        xrp = ctx.enter_context(tc.tile_pool(name="xrp", bufs=4))
-        rawp = ctx.enter_context(tc.tile_pool(name="rawp", bufs=RAW_BUFS))
-        gp = ctx.enter_context(tc.tile_pool(name="gp", bufs=3))
-        cp = ctx.enter_context(tc.tile_pool(name="cp", bufs=3))
-        sp = ctx.enter_context(tc.tile_pool(name="sp", bufs=4))
-        hpp = ctx.enter_context(tc.tile_pool(name="hpp", bufs=2))
-        hgp = ctx.enter_context(tc.tile_pool(name="hgp", bufs=2))
-        op = ctx.enter_context(tc.tile_pool(name="op", bufs=4))
-        olp = ctx.enter_context(tc.tile_pool(name="olp", bufs=2))
-        tp = ctx.enter_context(tc.psum_pool(name="tp", bufs=4))
-        accp = ctx.enter_context(tc.psum_pool(name="accp", bufs=4))
+        x_pool = ctx.enter_context(tc.tile_pool(name="x_pool", bufs=4))
+        raw_pool = ctx.enter_context(tc.tile_pool(name="raw_pool", bufs=RAW_CHUNKS))
+        grouped_pool = ctx.enter_context(tc.tile_pool(name="grouped_pool", bufs=3))
+        code_pool = ctx.enter_context(tc.tile_pool(name="code_pool", bufs=3))
+        silu_pool = ctx.enter_context(tc.tile_pool(name="silu_pool", bufs=4))
+        plane_pool = ctx.enter_context(tc.tile_pool(name="plane_pool", bufs=2))
+        h_pool = ctx.enter_context(tc.tile_pool(name="h_pool", bufs=2))
+        out_pool = ctx.enter_context(tc.tile_pool(name="out_pool", bufs=4))
+        tail_pool = ctx.enter_context(tc.tile_pool(name="tail_pool", bufs=2))
+        t_psum = ctx.enter_context(tc.psum_pool(name="t_psum", bufs=T_BANKS))
+        mx_psum = ctx.enter_context(tc.psum_pool(name="mx_psum", bufs=8 - T_BANKS))
         ctx.enter_context(tc.manual_schedule())
 
-        zeros = keep.tile([P, 512], BF16)
-        nc.vector.memset(zeros[:], 0.0)
-        ident = keep.tile([P, P], F32)
-        make_identity(nc, ident[:])
+        identity = keep.tile([P, P], F32)
+        make_identity(nc, identity[:])
         warm_in = keep.tile([P, 1], F32)
         warm_out = keep.tile([P, 1], F32)
         nc.vector.memset(warm_in[:], 0.0)
         nc.scalar.activation(out=warm_out[:], in_=warm_in[:], func=SILU)
 
-        xc = keep.tile([P, 1024], U32, align_bytes=64)
-        xs = keep.tile([P, 1024], U8, align_bytes=64)
-        hc = keep.tile([P, 6, 512], U32, align_bytes=64)
-        hs = keep.tile([P, 6, 512], U8, align_bytes=64)
+        x_codes = keep.tile([P, 2 * TOKENS], U32, align_bytes=64)
+        x_scales = keep.tile([P, 2 * TOKENS], U8, align_bytes=64)
+        h_codes = keep.tile([P, N_PASSES_2, TOKENS], U32, align_bytes=64)
+        h_scales = keep.tile([P, N_PASSES_2, TOKENS], U8, align_bytes=64)
 
-        xr32 = []
+        x_pairs = []
         for i in range(4):
-            xr = xrp.tile([P, D], BF16, tag="xr")
-            nc.sync.dma_start(out=xr[:], in_=xf[P * i : P * i + P, :])
-            xr32.append(xr[:].bitcast(F32))
+            x_raw = x_pool.tile([P, D_MODEL], BF16, tag="x_raw")
+            nc.sync.dma_start(out=x_raw[:], in_=x_rows[P * i : P * i + P, :])
+            x_pairs.append(x_raw[:].bitcast(F32))
 
-        raw32 = {}
+        raw_pairs = {}
 
         def load_chunk(c):
-            raw = rawp.tile([P, 4096], BF16, tag="raw")
-            if c < N_WIN:
-                nc.sync.dma_start(out=raw[:, 0:2048], in_=w1v[c])
-                nc.sync.dma_start(out=raw[:, 2048:4096], in_=w2v[c])
+            raw = raw_pool.tile([P, 4096], BF16, tag="raw")
+            if c < N_WINDOWS:
+                nc.sync.dma_start(out=raw[:, 0:2048], in_=w1_windows[c])
+                nc.sync.dma_start(out=raw[:, 2048:4096], in_=w2_windows[c])
             else:
-                b = c - N_WIN
+                b = c - N_WINDOWS
                 nc.sync.dma_start(
-                    out=raw[:].rearrange("p (j c) -> p j c", j=4),
-                    in_=w3v[b // 3, b % 3],
+                    out=raw[:].rearrange("p (j c) -> p j c", j=4), in_=w3_chunks[b // 3, b % 3]
                 )
-            raw32[c] = raw[:].bitcast(F32)
+            raw_pairs[c] = raw[:].bitcast(F32)
 
-        for c in range(RAW_BUFS):
+        for c in range(RAW_CHUNKS):
             load_chunk(c)
 
-        idle = accp.tile([P, 512], F32, tag="acc")
-
-        def keep_clock(n):
-            for k in range(n):
-                nc.tensor.matmul(
-                    out=idle[:], lhsT=zeros[:, 0:P], rhs=zeros[:], start=True, stop=True
-                )
-
-        def transpose_bunch(src, vector_banks, block_of=None, fill=0):
-            g = gp.tile([P, 4096], BF16, tag="g", align_bytes=64)
-            g32 = g[:].bitcast(F32)
+        def transpose_run(source, n_banks, blocks=None, vector_banks=()):
+            grouped = grouped_pool.tile([P, 1024 * n_banks], BF16, tag="grouped", align_bytes=64)
+            grouped_pairs = grouped[:].bitcast(F32)
             banks = []
-            for bank in range(4):
-                xt = tp.tile([P, 2, 256], F32, tag="xt")
+
+            def copy_out(bank):
+                block = bank if blocks is None else blocks[bank]
+                dst = grouped_pairs[:, BANK * block : BANK * block + BANK].rearrange("p (r u) -> p r u", u=2)
+                src = banks[bank][:].rearrange("p u r -> p r u")
+                if bank in vector_banks:
+                    nc.vector.tensor_copy(out=dst, in_=src)
+                else:
+                    nc.scalar.copy(out=dst, in_=src)
+
+            for bank in range(n_banks):
+                if bank >= T_BANKS:
+                    copy_out(bank - T_BANKS)
+                t_bank = t_psum.tile([P, 2, 256], F32, tag="t_bank")
                 for c in range(2):
                     for u in range(2):
-                        nc.tensor.transpose(
-                            xt[:, u, P * c : P * c + P], src(bank, u, c), ident[:]
-                        )
-                banks.append(xt)
-                if bank % 2 == 1:
-                    keep_clock(fill)
-            for bank in range(4):
-                blk = bank if block_of is None else block_of[bank]
-                dst = g32[:, 512 * blk : 512 * blk + 512].rearrange(
-                    "p (r u) -> p r u", u=2
-                )
-                srcv = banks[bank][:].rearrange("p u r -> p r u")
-                if bank in vector_banks:
-                    nc.vector.tensor_copy(out=dst, in_=srcv)
-                else:
-                    nc.scalar.copy(out=dst, in_=srcv)
-            return g
+                        nc.tensor.transpose(t_bank[:, u, P * c : P * c + P], source(bank, u, c), identity[:])
+                banks.append(t_bank)
+            for bank in range(n_banks - T_BANKS, n_banks):
+                copy_out(bank)
+            return grouped
 
-        def quantise(g, codes, scales, pieces=2):
-            w = 1024 // pieces
-            for h in range(pieces):
+        def quantise(grouped, codes, scales, pieces, words):
+            for q in range(pieces):
                 nc.vector.quantize_mx(
-                    out=codes[:, w * h : w * h + w].bitcast(FP8X4),
-                    scales=scales[:, w * h : w * h + w],
-                    in_=g[:, 4 * w * h : 4 * w * h + 4 * w],
+                    out=codes[:, words * q : words * q + words].bitcast(FP8X4),
+                    scales=scales[:, words * q : words * q + words],
+                    in_=grouped[:, 4 * words * q : 4 * words * q + 4 * words],
                 )
 
-        def x_src(bank, u, c):
-            off = (bank % 2) * 256 + u * P
-            return xr32[2 * (bank // 2) + c][:, off : off + P]
-
-        def w_src(v):
-            def src(bank, u, c):
-                off = (bank // 2) * 1024 + c * 512 + (bank % 2) * 256 + u * P
-                return raw32[v][:, off : off + P]
-
-            return src
-
-        def w3_src(b):
-            def src(bank, u, c):
-                off = (2 * (bank % 2) + c) * 512 + (bank // 2) * 256 + u * P
-                return raw32[N_WIN + b][:, off : off + P]
-
-            return src
-
-        def new_codes():
-            codes = cp.tile([P, 1024], U32, tag="codes", align_bytes=64)
-            scales = cp.tile([P, 1024], U8, tag="scales", align_bytes=64)
+        def new_codes(words):
+            codes = code_pool.tile([P, words], U32, tag="codes", align_bytes=64)
+            scales = code_pool.tile([P, words], U8, tag="scales", align_bytes=64)
             return codes, scales
 
-        def gate_up_pass(acc, cs, e, w, gk):
-            col = (2 * w + gk) * 256 + P * e
-            nc.tensor.matmul_mx(
-                out=acc[:],
-                lhsT=cs[0][:, col : col + P].bitcast(FP8X4),
-                lhsT_scale=cs[1][:, col : col + P],
-                rhs=xc[:, 512 * gk : 512 * gk + 512].bitcast(FP8X4),
-                rhs_scale=xs[:, 512 * gk : 512 * gk + 512],
-                start=(gk == 0),
-                stop=(gk == 1),
-            )
+        def x_source(bank, u, c):
+            first = (bank % 2) * 256 + u * P
+            return x_pairs[2 * (bank // 2) + c][:, first : first + P]
 
-        def gate_up(cs):
-            accs = {}
-            for e in range(2):
-                for w in range(2):
-                    acc = accp.tile([P, 512], F32, tag="acc")
-                    for gk in range(2):
-                        gate_up_pass(acc, cs, e, w, gk)
-                    accs[(e, w)] = acc
-            return accs
+        def window_source(v):
+            def source(bank, u, c):
+                first = (bank // 2) * 1024 + c * 512 + (bank % 2) * 256 + u * P
+                return raw_pairs[v][:, first : first + P]
 
-        def gate_up_first(cs):
-            accs = {}
-            for w in range(2):
-                for e in range(2):
-                    acc = accp.tile([P, 512], F32, tag="acc")
-                    accs[(e, w)] = acc
-                for gk in range(2):
-                    for e in range(2):
-                        gate_up_pass(accs[(e, w)], cs, e, w, gk)
-            return accs
+            return source
 
-        def silu(accs):
-            ss = []
-            for e in range(2):
-                s = sp.tile([P, 512], F32, tag="s")
-                nc.scalar.activation(out=s[:], in_=accs[(e, 0)][:], func=SILU)
-                ss.append(s)
-            return ss
+        def run_source(run):
+            def source(bank, u, c):
+                g = 3 * (run % 2) + bank // 2
+                first = (2 * (bank % 2) + c) * 512 + (g % 2) * 256 + u * P
+                return raw_pairs[N_WINDOWS + 3 * (run // 2) + g // 2][:, first : first + P]
 
-        def quantise_h(hg, g):
+            return source
+
+        def gate_up(window_codes, order):
+            codes, scales = window_codes
+            sums = {}
+            for e, w, g in order:
+                if g == 0:
+                    acc = mx_psum.tile([P, BANK], F32, tag="acc")
+                    sums[(e, w)] = acc
+                first = (2 * w + g) * 256 + P * e
+                nc.tensor.matmul_mx(
+                    out=sums[(e, w)][:],
+                    lhsT=codes[:, first : first + P].bitcast(FP8X4),
+                    lhsT_scale=scales[:, first : first + P],
+                    rhs=x_codes[:, TOKENS * g : TOKENS * g + TOKENS].bitcast(FP8X4),
+                    rhs_scale=x_scales[:, TOKENS * g : TOKENS * g + TOKENS],
+                    start=(g == 0),
+                    stop=(g == 1),
+                )
+            return sums
+
+        by_f_tile = [(e, w, g) for e in range(2) for w in range(2) for g in range(2)]
+        by_bank = [(e, w, g) for w in range(2) for g in range(2) for e in range(2)]
+
+        def quantise_h(grouped_h, g):
             nc.vector.quantize_mx(
-                out=hc[:, g, :].bitcast(FP8X4),
-                scales=hs[:, g, :],
-                in_=hg[:].rearrange("p w t -> p (w t)"),
+                out=h_codes[:, g, :].bitcast(FP8X4),
+                scales=h_scales[:, g, :],
+                in_=grouped_h[:].rearrange("p n t -> p (n t)"),
             )
 
-        state = {"hp": None, "pending": None}
+        grouped = transpose_run(x_source, 4, blocks=(0, 2, 1, 3))
+        quantise(grouped, x_codes, x_scales, pieces=2, words=TOKENS)
+        grouped = transpose_run(window_source(0), 4)
+        window_codes = new_codes(1024)
+        quantise(grouped, window_codes[0], window_codes[1], pieces=4, words=256)
 
-        def flush_pending():
-            if state["pending"] is not None:
-                quantise_h(state["pending"][0], state["pending"][1])
-                state["pending"] = None
+        planes = None
+        waiting = None
+        for v in range(N_WINDOWS):
+            if v == 0:
+                sums = gate_up(window_codes, by_bank)
+            if v + 1 < N_WINDOWS:
+                grouped = transpose_run(window_source(v + 1), 4, vector_banks=(1, 3) if v == 0 else ())
+            else:
+                grouped = transpose_run(run_source(0), 6)
+            if v + RAW_CHUNKS < N_CHUNKS:
+                load_chunk(v + RAW_CHUNKS)
+            if v > 0:
+                sums = gate_up(window_codes, by_f_tile)
 
-        def gate(v, ss, accs):
+            silus = []
+            for e in range(2):
+                silu_a = silu_pool.tile([P, BANK], F32, tag="silu_a")
+                nc.scalar.activation(out=silu_a[:], in_=sums[(e, 0)][:], func=SILU)
+                silus.append(silu_a)
+
+            if v + 1 < N_WINDOWS:
+                window_codes = new_codes(1024)
+                quantise(grouped, window_codes[0], window_codes[1], pieces=2, words=512)
+            else:
+                run_codes = {0: new_codes(1536)}
+                quantise(grouped, run_codes[0][0], run_codes[0][1], pieces=3, words=512)
+            if waiting is not None:
+                quantise_h(waiting[0], waiting[1])
+                waiting = None
+
             if v % 2 == 0:
-                hp = hpp.tile([P, 4, 512], BF16, tag="hp")
-                state["hp"] = hp
-            hp = state["hp"]
+                planes = plane_pool.tile([P, 4, TOKENS], BF16, tag="planes")
             for e in range(2):
                 nc.vector.tensor_tensor(
-                    out=hp[:, 2 * (v % 2) + e, :],
-                    in0=ss[e][:],
-                    in1=accs[(e, 1)][:],
-                    op=MULT,
+                    out=planes[:, 2 * (v % 2) + e, :], in0=silus[e][:], in1=sums[(e, 1)][:], op=MULT
                 )
             if v % 2 == 1:
-                hg = hgp.tile([P, 512, 4], BF16, tag="hg", align_bytes=64)
+                grouped_h = h_pool.tile([P, TOKENS, 4], BF16, tag="grouped_h", align_bytes=64)
                 nc.vector.tensor_copy(
-                    out=hg[:].rearrange("p (c i) t -> p c t i", i=4),
-                    in_=hp[:].rearrange("p t (c i) -> p c t i", i=4),
+                    out=grouped_h[:].rearrange("p (n i) t -> p n t i", i=4),
+                    in_=planes[:].rearrange("p t (n i) -> p n t i", i=4),
                 )
-                state["pending"] = (hg, v // 2)
+                waiting = (grouped_h, v // 2)
 
-        keep_clock(WARM)
-        gx = transpose_bunch(x_src, (), block_of=(0, 2, 1, 3), fill=1)
-        quantise(gx, xc, xs)
-        g0 = transpose_bunch(w_src(0), (), fill=1)
-        cur = new_codes()
-        quantise(g0, cur[0], cur[1], pieces=4)
-        accs = gate_up_first(cur)
-        gn = transpose_bunch(w_src(1), (1, 3))
-        load_chunk(RAW_BUFS)
-        ss = silu(accs)
-        cur = new_codes()
-        quantise(gn, cur[0], cur[1])
-        gate(0, ss, accs)
-
-        for v in range(1, N_WIN):
-            if v + 1 < N_WIN:
-                gn = transpose_bunch(w_src(v + 1), ())
-            else:
-                gn = transpose_bunch(w3_src(0), ())
-            if v + RAW_BUFS < N_CHUNK:
-                load_chunk(v + RAW_BUFS)
-            accs = gate_up(cur)
-            ss = silu(accs)
-            cur = new_codes()
-            quantise(gn, cur[0], cur[1])
-            flush_pending()
-            gate(v, ss, accs)
-
-        def down_pass(acc, i, g, cs, col, n):
+        def down_pass(acc, i, g, first, n):
+            codes, scales = run_codes[2 * (first // BANK) + g // 3]
+            col = BANK * (g % 3) + first % BANK
             nc.tensor.matmul_mx(
                 out=acc,
-                lhsT=hc[:, g, P * i : P * i + P].bitcast(FP8X4),
-                lhsT_scale=hs[:, g, P * i : P * i + P],
-                rhs=cs[0][:, col : col + n].bitcast(FP8X4),
-                rhs_scale=cs[1][:, col : col + n],
+                lhsT=h_codes[:, g, P * i : P * i + P].bitcast(FP8X4),
+                lhsT_scale=h_scales[:, g, P * i : P * i + P],
+                rhs=codes[:, col : col + n].bitcast(FP8X4),
+                rhs_scale=scales[:, col : col + n],
                 start=(g == 0),
-                stop=(g == 5),
+                stop=(g == N_PASSES_2 - 1),
             )
 
-        def store(i, acc, half, on_vector):
-            o = op.tile([P, 512], F32, tag="o")
-            if on_vector:
-                nc.vector.tensor_copy(out=o[:], in_=acc[:])
-            else:
-                nc.scalar.copy(out=o[:], in_=acc[:])
-            nc.sync.dma_start(
-                out=of[P * i : P * i + P, 512 * half : 512 * half + 512], in_=o[:]
-            )
-
-        w3codes = {0: cur}
-        acc2 = None
-        for b in range(N_W3):
-            half, gpair = b // 3, b % 3
-            n_tok = 4 if half == 0 else 3
-            if b + 1 < N_W3:
-                gn = transpose_bunch(w3_src(b + 1), (1, 3))
-            if gpair == 0:
-                acc2 = []
-                for i in range(n_tok):
-                    acc = accp.tile([P, 512], F32, tag="acc")
-                    acc2.append(acc)
-            flush_pending()
-            for i in range(n_tok):
-                for gl in range(2):
-                    down_pass(acc2[i][:], i, 2 * gpair + gl, w3codes[b], 512 * gl, 512)
-            if b + 1 < N_W3:
-                w3codes[b + 1] = new_codes()
-                quantise(gn, w3codes[b + 1][0], w3codes[b + 1][1])
-            if gpair == 2:
-                for i in range(n_tok):
-                    store(i, acc2[i], half, i % 2 == 1)
+        sums = None
+        for run in range(N_RUNS):
+            half, part = run // 2, run % 2
+            n_tiles = 4 if half == 0 else 3
+            if run + 1 < N_RUNS:
+                grouped = transpose_run(run_source(run + 1), 6)
+            if part == 0:
+                sums = []
+                for i in range(n_tiles):
+                    acc = mx_psum.tile([P, BANK], F32, tag="acc")
+                    sums.append(acc)
+            if waiting is not None:
+                quantise_h(waiting[0], waiting[1])
+                waiting = None
+            for i in range(n_tiles):
+                for g in range(3 * part, 3 * part + 3):
+                    down_pass(sums[i][:], i, g, BANK * half, BANK)
+            if run + 1 < N_RUNS:
+                run_codes[run + 1] = new_codes(1536)
+                quantise(grouped, run_codes[run + 1][0], run_codes[run + 1][1], pieces=3, words=512)
+            if part == 1:
+                for i in range(n_tiles):
+                    result = out_pool.tile([P, BANK], F32, tag="result")
+                    if i % 2 == 0:
+                        nc.scalar.copy(out=result[:], in_=sums[i][:])
+                    else:
+                        nc.vector.tensor_copy(out=result[:], in_=sums[i][:])
+                    nc.sync.dma_start(
+                        out=out_rows[P * i : P * i + P, BANK * half : BANK * half + BANK], in_=result[:]
+                    )
 
         for q in range(2):
-            last = tp.tile([P, 2, 256], F32, tag="xt")
-            for g in range(6):
-                down_pass(last[:, 0, :], 3, g, w3codes[3 + g // 2], 512 * (g % 2) + 256 * q, 256)
-            ol = olp.tile([P, 256], F32, tag="ol")
+            first = BANK + 256 * q
+            t_bank = t_psum.tile([P, 2, 256], F32, tag="t_bank")
+            for g in range(N_PASSES_2):
+                down_pass(t_bank[:, 0, :], 3, g, first, 256)
+            result = tail_pool.tile([P, 256], F32, tag="tail_result")
             if q == 0:
-                nc.vector.tensor_copy(out=ol[:], in_=last[:, 0, :])
+                nc.vector.tensor_copy(out=result[:], in_=t_bank[:, 0, :])
             else:
-                nc.scalar.copy(out=ol[:], in_=last[:, 0, :])
-            nc.sync.dma_start(
-                out=of[3 * P : 4 * P, 512 + 256 * q : 512 + 256 * q + 256], in_=ol[:]
-            )
+                nc.scalar.copy(out=result[:], in_=t_bank[:, 0, :])
+            nc.sync.dma_start(out=out_rows[3 * P : 4 * P, first : first + 256], in_=result[:])

@@ -21,9 +21,9 @@ BANK = 512
 T_BANKS = 4
 N_WINDOWS = D_FF // 256
 N_PASSES_2 = D_FF // 512
-N_RUNS = 4
+N_RUNS = 6
 N_CHUNKS = N_WINDOWS + 6
-RAW_CHUNKS = 12
+RAW_CHUNKS = 14
 
 
 def tile_nf4mlp_kernel(tc, x, weight1, weight2, weight3, out):
@@ -136,9 +136,8 @@ def tile_nf4mlp_kernel(tc, x, weight1, weight2, weight3, out):
 
         def run_source(run):
             def source(bank, u, c):
-                g = 3 * (run % 2) + bank // 2
-                first = (2 * (bank % 2) + c) * 512 + (g % 2) * 256 + u * P
-                return raw_pairs[N_WINDOWS + 3 * (run // 2) + g // 2][:, first : first + P]
+                first = (2 * (bank % 2) + c) * 512 + (bank // 2) * 256 + u * P
+                return raw_pairs[N_WINDOWS + run][:, first : first + P]
 
             return source
 
@@ -185,7 +184,7 @@ def tile_nf4mlp_kernel(tc, x, weight1, weight2, weight3, out):
             if v + 1 < N_WINDOWS:
                 grouped = transpose_run(window_source(v + 1), 4, vector_banks=(1, 3) if v == 0 else ())
             else:
-                grouped = transpose_run(run_source(0), 6)
+                grouped = transpose_run(run_source(0), 4)
             if v + RAW_CHUNKS < N_CHUNKS:
                 load_chunk(v + RAW_CHUNKS)
             if v > 0:
@@ -197,12 +196,8 @@ def tile_nf4mlp_kernel(tc, x, weight1, weight2, weight3, out):
                 nc.scalar.activation(out=silu_a[:], in_=sums[(e, 0)][:], func=SILU)
                 silus.append(silu_a)
 
-            if v + 1 < N_WINDOWS:
-                window_codes = new_codes(1024)
-                quantise(grouped, window_codes[0], window_codes[1], pieces=2, words=512)
-            else:
-                run_codes = {0: new_codes(1536)}
-                quantise(grouped, run_codes[0][0], run_codes[0][1], pieces=3, words=512)
+            window_codes = new_codes(1024)
+            quantise(grouped, window_codes[0], window_codes[1], pieces=2, words=512)
             if waiting is not None:
                 quantise_h(waiting[0], waiting[1])
                 waiting = None
@@ -222,8 +217,8 @@ def tile_nf4mlp_kernel(tc, x, weight1, weight2, weight3, out):
                 waiting = (grouped_h, v // 2)
 
         def down_pass(acc, i, g, first, n):
-            codes, scales = run_codes[2 * (first // BANK) + g // 3]
-            col = BANK * (g % 3) + first % BANK
+            codes, scales = run_codes[3 * (first // BANK) + g // 2]
+            col = BANK * (g % 2) + first % BANK
             nc.tensor.matmul_mx(
                 out=acc,
                 lhsT=h_codes[:, g, P * i : P * i + P].bitcast(FP8X4),
@@ -234,12 +229,13 @@ def tile_nf4mlp_kernel(tc, x, weight1, weight2, weight3, out):
                 stop=(g == N_PASSES_2 - 1),
             )
 
+        run_codes = {0: window_codes}
         sums = None
         for run in range(N_RUNS):
-            half, part = run // 2, run % 2
+            half, part = run // 3, run % 3
             n_tiles = 4 if half == 0 else 3
             if run + 1 < N_RUNS:
-                grouped = transpose_run(run_source(run + 1), 6)
+                grouped = transpose_run(run_source(run + 1), 4, vector_banks=(1, 3))
             if part == 0:
                 sums = []
                 for i in range(n_tiles):
@@ -249,12 +245,12 @@ def tile_nf4mlp_kernel(tc, x, weight1, weight2, weight3, out):
                 quantise_h(waiting[0], waiting[1])
                 waiting = None
             for i in range(n_tiles):
-                for g in range(3 * part, 3 * part + 3):
+                for g in range(2 * part, 2 * part + 2):
                     down_pass(sums[i][:], i, g, BANK * half, BANK)
             if run + 1 < N_RUNS:
-                run_codes[run + 1] = new_codes(1536)
-                quantise(grouped, run_codes[run + 1][0], run_codes[run + 1][1], pieces=3, words=512)
-            if part == 1:
+                run_codes[run + 1] = new_codes(1024)
+                quantise(grouped, run_codes[run + 1][0], run_codes[run + 1][1], pieces=2, words=512)
+            if part == 2:
                 for i in range(n_tiles):
                     result = out_pool.tile([P, BANK], F32, tag="result")
                     if i % 2 == 0:

@@ -19,10 +19,11 @@ FLOPS = 2 * TOKENS * D_MODEL * D_FF * 3
 
 BANK = 512
 T_BANKS = 4
+CHUNK_WORDS = 256 * T_BANKS
 N_WINDOWS = D_FF // 256
 N_PASSES_2 = D_FF // 512
-N_RUNS = 6
-N_CHUNKS = N_WINDOWS + 6
+N_PARTS = 6
+N_CHUNKS = N_WINDOWS + N_PARTS
 RAW_CHUNKS = 14
 
 
@@ -32,7 +33,7 @@ def tile_nf4mlp_kernel(tc, x, weight1, weight2, weight3, out):
     out_rows = out.flatten_outer_dims()
     w1_windows = weight1.rearrange("(v r e) k -> v r (e k)", r=P, e=2)
     w2_windows = weight2.rearrange("(v r e) k -> v r (e k)", r=P, e=2)
-    w3_chunks = weight3.rearrange("(half j p) (b c) -> half b p j c", j=4, p=P, c=1024)
+    w3_parts = weight3.rearrange("(half j p) (b c) -> half b p j c", j=4, p=P, c=1024)
 
     with ExitStack() as ctx:
         keep = ctx.enter_context(tc.tile_pool(name="keep", bufs=1))
@@ -75,42 +76,37 @@ def tile_nf4mlp_kernel(tc, x, weight1, weight2, weight3, out):
                 nc.sync.dma_start(out=raw[:, 0:2048], in_=w1_windows[c])
                 nc.sync.dma_start(out=raw[:, 2048:4096], in_=w2_windows[c])
             else:
-                b = c - N_WINDOWS
+                part = c - N_WINDOWS
                 nc.sync.dma_start(
-                    out=raw[:].rearrange("p (j c) -> p j c", j=4), in_=w3_chunks[b // 3, b % 3]
+                    out=raw[:].rearrange("p (j c) -> p j c", j=4), in_=w3_parts[part // 3, part % 3]
                 )
             raw_pairs[c] = raw[:].bitcast(F32)
 
         for c in range(RAW_CHUNKS):
             load_chunk(c)
 
-        def transpose_run(source, n_banks, blocks=None, vector_banks=()):
-            grouped = grouped_pool.tile([P, 1024 * n_banks], BF16, tag="grouped", align_bytes=64)
+        def transpose_run(source, blocks=(0, 1, 2, 3), vector_banks=()):
+            grouped = grouped_pool.tile([P, 4 * CHUNK_WORDS], BF16, tag="grouped", align_bytes=64)
             grouped_pairs = grouped[:].bitcast(F32)
             banks = []
-
-            def copy_out(bank):
-                block = bank if blocks is None else blocks[bank]
-                dst = grouped_pairs[:, BANK * block : BANK * block + BANK].rearrange("p (r u) -> p r u", u=2)
-                src = banks[bank][:].rearrange("p u r -> p r u")
-                if bank in vector_banks:
-                    nc.vector.tensor_copy(out=dst, in_=src)
-                else:
-                    nc.scalar.copy(out=dst, in_=src)
-
-            for bank in range(n_banks):
-                if bank >= T_BANKS:
-                    copy_out(bank - T_BANKS)
+            for bank in range(T_BANKS):
                 t_bank = t_psum.tile([P, 2, 256], F32, tag="t_bank")
                 for c in range(2):
                     for u in range(2):
                         nc.tensor.transpose(t_bank[:, u, P * c : P * c + P], source(bank, u, c), identity[:])
                 banks.append(t_bank)
-            for bank in range(n_banks - T_BANKS, n_banks):
-                copy_out(bank)
+            for bank in range(T_BANKS):
+                first = BANK * blocks[bank]
+                dst = grouped_pairs[:, first : first + BANK].rearrange("p (r u) -> p r u", u=2)
+                src = banks[bank][:].rearrange("p u r -> p r u")
+                if bank in vector_banks:
+                    nc.vector.tensor_copy(out=dst, in_=src)
+                else:
+                    nc.scalar.copy(out=dst, in_=src)
             return grouped
 
-        def quantise(grouped, codes, scales, pieces, words):
+        def quantise(grouped, codes, scales, pieces):
+            words = CHUNK_WORDS // pieces
             for q in range(pieces):
                 nc.vector.quantize_mx(
                     out=codes[:, words * q : words * q + words].bitcast(FP8X4),
@@ -118,9 +114,9 @@ def tile_nf4mlp_kernel(tc, x, weight1, weight2, weight3, out):
                     in_=grouped[:, 4 * words * q : 4 * words * q + 4 * words],
                 )
 
-        def new_codes(words):
-            codes = code_pool.tile([P, words], U32, tag="codes", align_bytes=64)
-            scales = code_pool.tile([P, words], U8, tag="scales", align_bytes=64)
+        def new_codes():
+            codes = code_pool.tile([P, CHUNK_WORDS], U32, tag="codes", align_bytes=64)
+            scales = code_pool.tile([P, CHUNK_WORDS], U8, tag="scales", align_bytes=64)
             return codes, scales
 
         def x_source(bank, u, c):
@@ -134,16 +130,15 @@ def tile_nf4mlp_kernel(tc, x, weight1, weight2, weight3, out):
 
             return source
 
-        def run_source(run):
+        def part_source(part):
             def source(bank, u, c):
                 first = (2 * (bank % 2) + c) * 512 + (bank // 2) * 256 + u * P
-                return raw_pairs[N_WINDOWS + run][:, first : first + P]
+                return raw_pairs[N_WINDOWS + part][:, first : first + P]
 
             return source
 
-        def gate_up(window_codes, order):
+        def gate_up(window_codes, order, sums):
             codes, scales = window_codes
-            sums = {}
             for e, w, g in order:
                 if g == 0:
                     acc = mx_psum.tile([P, BANK], F32, tag="acc")
@@ -158,10 +153,9 @@ def tile_nf4mlp_kernel(tc, x, weight1, weight2, weight3, out):
                     start=(g == 0),
                     stop=(g == 1),
                 )
-            return sums
 
         by_f_tile = [(e, w, g) for e in range(2) for w in range(2) for g in range(2)]
-        by_bank = [(e, w, g) for w in range(2) for g in range(2) for e in range(2)]
+        by_weight = [(e, w, g) for w in range(2) for g in range(2) for e in range(2)]
 
         def quantise_h(grouped_h, g):
             nc.vector.quantize_mx(
@@ -170,25 +164,28 @@ def tile_nf4mlp_kernel(tc, x, weight1, weight2, weight3, out):
                 in_=grouped_h[:].rearrange("p n t -> p (n t)"),
             )
 
-        grouped = transpose_run(x_source, 4, blocks=(0, 2, 1, 3))
-        quantise(grouped, x_codes, x_scales, pieces=2, words=TOKENS)
-        grouped = transpose_run(window_source(0), 4)
-        window_codes = new_codes(1024)
-        quantise(grouped, window_codes[0], window_codes[1], pieces=4, words=256)
+        grouped = transpose_run(x_source, blocks=(0, 2, 1, 3))
+        quantise(grouped, x_codes, x_scales, pieces=2)
+        grouped = transpose_run(window_source(0))
+        chunk_codes = new_codes()
+        quantise(grouped, chunk_codes[0], chunk_codes[1], pieces=4)
 
         planes = None
         waiting = None
         for v in range(N_WINDOWS):
+            sums = {}
             if v == 0:
-                sums = gate_up(window_codes, by_bank)
-            if v + 1 < N_WINDOWS:
-                grouped = transpose_run(window_source(v + 1), 4, vector_banks=(1, 3) if v == 0 else ())
+                gate_up(chunk_codes, by_weight[:4], sums)
+                grouped = transpose_run(window_source(1), vector_banks=(1, 3))
+                gate_up(chunk_codes, by_weight[4:], sums)
             else:
-                grouped = transpose_run(run_source(0), 4)
+                if v + 1 < N_WINDOWS:
+                    grouped = transpose_run(window_source(v + 1))
+                else:
+                    grouped = transpose_run(part_source(0))
+                gate_up(chunk_codes, by_f_tile, sums)
             if v + RAW_CHUNKS < N_CHUNKS:
                 load_chunk(v + RAW_CHUNKS)
-            if v > 0:
-                sums = gate_up(window_codes, by_f_tile)
 
             silus = []
             for e in range(2):
@@ -196,8 +193,8 @@ def tile_nf4mlp_kernel(tc, x, weight1, weight2, weight3, out):
                 nc.scalar.activation(out=silu_a[:], in_=sums[(e, 0)][:], func=SILU)
                 silus.append(silu_a)
 
-            window_codes = new_codes(1024)
-            quantise(grouped, window_codes[0], window_codes[1], pieces=2, words=512)
+            chunk_codes = new_codes()
+            quantise(grouped, chunk_codes[0], chunk_codes[1], pieces=2)
             if waiting is not None:
                 quantise_h(waiting[0], waiting[1])
                 waiting = None
@@ -216,8 +213,10 @@ def tile_nf4mlp_kernel(tc, x, weight1, weight2, weight3, out):
                 )
                 waiting = (grouped_h, v // 2)
 
+        part_codes = {0: chunk_codes}
+
         def down_pass(acc, i, g, first, n):
-            codes, scales = run_codes[3 * (first // BANK) + g // 2]
+            codes, scales = part_codes[3 * (first // BANK) + g // 2]
             col = BANK * (g % 2) + first % BANK
             nc.tensor.matmul_mx(
                 out=acc,
@@ -229,34 +228,33 @@ def tile_nf4mlp_kernel(tc, x, weight1, weight2, weight3, out):
                 stop=(g == N_PASSES_2 - 1),
             )
 
-        run_codes = {0: window_codes}
-        sums = None
-        for run in range(N_RUNS):
-            half, part = run // 3, run % 3
+        tile_sums = None
+        for part in range(N_PARTS):
+            half, pair = part // 3, part % 3
             n_tiles = 4 if half == 0 else 3
-            if run + 1 < N_RUNS:
-                grouped = transpose_run(run_source(run + 1), 4, vector_banks=(1, 3))
-            if part == 0:
-                sums = []
+            if part + 1 < N_PARTS:
+                grouped = transpose_run(part_source(part + 1), vector_banks=(1, 3))
+            if pair == 0:
+                tile_sums = []
                 for i in range(n_tiles):
                     acc = mx_psum.tile([P, BANK], F32, tag="acc")
-                    sums.append(acc)
+                    tile_sums.append(acc)
             if waiting is not None:
                 quantise_h(waiting[0], waiting[1])
                 waiting = None
             for i in range(n_tiles):
-                for g in range(2 * part, 2 * part + 2):
-                    down_pass(sums[i][:], i, g, BANK * half, BANK)
-            if run + 1 < N_RUNS:
-                run_codes[run + 1] = new_codes(1024)
-                quantise(grouped, run_codes[run + 1][0], run_codes[run + 1][1], pieces=2, words=512)
-            if part == 2:
+                for g in range(2 * pair, 2 * pair + 2):
+                    down_pass(tile_sums[i][:], i, g, BANK * half, BANK)
+            if part + 1 < N_PARTS:
+                part_codes[part + 1] = new_codes()
+                quantise(grouped, part_codes[part + 1][0], part_codes[part + 1][1], pieces=2)
+            if pair == 2:
                 for i in range(n_tiles):
                     result = out_pool.tile([P, BANK], F32, tag="result")
                     if i % 2 == 0:
-                        nc.scalar.copy(out=result[:], in_=sums[i][:])
+                        nc.scalar.copy(out=result[:], in_=tile_sums[i][:])
                     else:
-                        nc.vector.tensor_copy(out=result[:], in_=sums[i][:])
+                        nc.vector.tensor_copy(out=result[:], in_=tile_sums[i][:])
                     nc.sync.dma_start(
                         out=out_rows[P * i : P * i + P, BANK * half : BANK * half + BANK], in_=result[:]
                     )

from contextlib import ExitStack

import concourse.mybir as mybir
from concourse.masks import make_identity

F32 = mybir.dt.float32
BF16 = mybir.dt.bfloat16
U32 = mybir.dt.uint32
U8 = mybir.dt.uint8
FP8X4 = mybir.dt.float8_e4m3fn_x4
SILU = mybir.ActivationFunctionType.Silu
MULT = mybir.AluOpType.mult

P = 128
TOKENS = 512
D_MODEL = 1024
D_FF = 3072
FLOPS = 2 * TOKENS * D_MODEL * D_FF * 3

BANK = 512
T_BANKS = 4
CHUNK_WORDS = 256 * T_BANKS
N_WINDOWS = D_FF // 256
N_PASSES_2 = D_FF // 512
N_PARTS = 6
N_CHUNKS = N_WINDOWS + N_PARTS
RAW_CHUNKS = 14


def tile_nf4mlp_kernel(tc, x, weight1, weight2, weight3, out):
    nc = tc.nc
    x_rows = x.flatten_outer_dims()
    out_rows = out.flatten_outer_dims()
    w1_windows = weight1.rearrange("(v r e) k -> v r (e k)", r=P, e=2)
    w2_windows = weight2.rearrange("(v r e) k -> v r (e k)", r=P, e=2)
    w3_parts = weight3.rearrange("(half j p) (b c) -> half b p j c", j=4, p=P, c=1024)

    with ExitStack() as ctx:
        keep = ctx.enter_context(tc.tile_pool(name="keep", bufs=1))
        x_pool = ctx.enter_context(tc.tile_pool(name="x_pool", bufs=4))
        raw_pool = ctx.enter_context(tc.tile_pool(name="raw_pool", bufs=RAW_CHUNKS))
        grouped_pool = ctx.enter_context(tc.tile_pool(name="grouped_pool", bufs=3))
        code_pool = ctx.enter_context(tc.tile_pool(name="code_pool", bufs=3))
        silu_pool = ctx.enter_context(tc.tile_pool(name="silu_pool", bufs=4))
        plane_pool = ctx.enter_context(tc.tile_pool(name="plane_pool", bufs=2))
        h_pool = ctx.enter_context(tc.tile_pool(name="h_pool", bufs=2))
        out_pool = ctx.enter_context(tc.tile_pool(name="out_pool", bufs=4))
        tail_pool = ctx.enter_context(tc.tile_pool(name="tail_pool", bufs=2))
        t_psum = ctx.enter_context(tc.psum_pool(name="t_psum", bufs=T_BANKS))
        mx_psum = ctx.enter_context(tc.psum_pool(name="mx_psum", bufs=8 - T_BANKS))
        ctx.enter_context(tc.manual_schedule())

        identity = keep.tile([P, P], F32)
        make_identity(nc, identity[:])
        warm_in = keep.tile([P, 1], F32)
        warm_out = keep.tile([P, 1], F32)
        nc.vector.memset(warm_in[:], 0.0)
        nc.scalar.activation(out=warm_out[:], in_=warm_in[:], func=SILU)

        x_codes = keep.tile([P, 2 * TOKENS], U32, align_bytes=64)
        x_scales = keep.tile([P, 2 * TOKENS], U8, align_bytes=64)
        h_codes = keep.tile([P, N_PASSES_2, TOKENS], U32, align_bytes=64)
        h_scales = keep.tile([P, N_PASSES_2, TOKENS], U8, align_bytes=64)

        x_pairs = []
        for i in range(4):
            x_raw = x_pool.tile([P, D_MODEL], BF16, tag="x_raw")
            nc.sync.dma_start(out=x_raw[:], in_=x_rows[P * i : P * i + P, :])
            x_pairs.append(x_raw[:].bitcast(F32))

        raw_pairs = {}

        def load_chunk(c):
            raw = raw_pool.tile([P, 4096], BF16, tag="raw")
            if c < N_WINDOWS:
                nc.sync.dma_start(out=raw[:, 0:2048], in_=w1_windows[c])
                nc.sync.dma_start(out=raw[:, 2048:4096], in_=w2_windows[c])
            else:
                part = c - N_WINDOWS
                nc.sync.dma_start(
                    out=raw[:].rearrange("p (j c) -> p j c", j=4), in_=w3_parts[part // 3, part % 3]
                )
            raw_pairs[c] = raw[:].bitcast(F32)

        for c in range(RAW_CHUNKS):
            load_chunk(c)

        def transpose_run(source, blocks=(0, 1, 2, 3), vector_banks=()):
            grouped = grouped_pool.tile([P, 4 * CHUNK_WORDS], BF16, tag="grouped", align_bytes=64)
            grouped_pairs = grouped[:].bitcast(F32)
            banks = []
            for bank in range(T_BANKS):
                t_bank = t_psum.tile([P, 2, 256], F32, tag="t_bank")
                for c in range(2):
                    for u in range(2):
                        nc.tensor.transpose(t_bank[:, u, P * c : P * c + P], source(bank, u, c), identity[:])
                banks.append(t_bank)
            for bank in range(T_BANKS):
                first = BANK * blocks[bank]
                dst = grouped_pairs[:, first : first + BANK].rearrange("p (r u) -> p r u", u=2)
                src = banks[bank][:].rearrange("p u r -> p r u")
                if bank in vector_banks:
                    nc.vector.tensor_copy(out=dst, in_=src)
                else:
                    nc.scalar.copy(out=dst, in_=src)
            return grouped

        def quantise(grouped, codes, scales, pieces):
            words = CHUNK_WORDS // pieces
            for q in range(pieces):
                nc.vector.quantize_mx(
                    out=codes[:, words * q : words * q + words].bitcast(FP8X4),
                    scales=scales[:, words * q : words * q + words],
                    in_=grouped[:, 4 * words * q : 4 * words * q + 4 * words],
                )

        def new_codes():
            codes = code_pool.tile([P, CHUNK_WORDS], U32, tag="codes", align_bytes=64)
            scales = code_pool.tile([P, CHUNK_WORDS], U8, tag="scales", align_bytes=64)
            return codes, scales

        def x_source(bank, u, c):
            first = (bank % 2) * 256 + u * P
            return x_pairs[2 * (bank // 2) + c][:, first : first + P]

        def window_source(v):
            def source(bank, u, c):
                first = (bank // 2) * 1024 + c * 512 + (bank % 2) * 256 + u * P
                return raw_pairs[v][:, first : first + P]

            return source

        def part_source(part):
            def source(bank, u, c):
                first = (2 * (bank % 2) + c) * 512 + (bank // 2) * 256 + u * P
                return raw_pairs[N_WINDOWS + part][:, first : first + P]

            return source

        def gate_up(window_codes, order, sums):
            codes, scales = window_codes
            for e, w, g in order:
                if g == 0:
                    acc = mx_psum.tile([P, BANK], F32, tag="acc")
                    sums[(e, w)] = acc
                first = (2 * w + g) * 256 + P * e
                nc.tensor.matmul_mx(
                    out=sums[(e, w)][:],
                    lhsT=codes[:, first : first + P].bitcast(FP8X4),
                    lhsT_scale=scales[:, first : first + P],
                    rhs=x_codes[:, TOKENS * g : TOKENS * g + TOKENS].bitcast(FP8X4),
                    rhs_scale=x_scales[:, TOKENS * g : TOKENS * g + TOKENS],
                    start=(g == 0),
                    stop=(g == 1),
                )

        by_f_tile = [(e, w, g) for e in range(2) for w in range(2) for g in range(2)]
        by_weight = [(e, w, g) for w in range(2) for g in range(2) for e in range(2)]

        def quantise_h(grouped_h, g):
            nc.vector.quantize_mx(
                out=h_codes[:, g, :].bitcast(FP8X4),
                scales=h_scales[:, g, :],
                in_=grouped_h[:].rearrange("p n t -> p (n t)"),
            )

        grouped = transpose_run(x_source, blocks=(0, 2, 1, 3))
        quantise(grouped, x_codes, x_scales, pieces=2)
        grouped = transpose_run(window_source(0))
        chunk_codes = new_codes()
        quantise(grouped, chunk_codes[0], chunk_codes[1], pieces=4)

        planes = None
        waiting = None
        for v in range(N_WINDOWS):
            sums = {}
            if v == 0:
                gate_up(chunk_codes, by_weight[:4], sums)
                grouped = transpose_run(window_source(1), vector_banks=(1, 3))
                gate_up(chunk_codes, by_weight[4:], sums)
            else:
                if v + 1 < N_WINDOWS:
                    grouped = transpose_run(window_source(v + 1))
                else:
                    grouped = transpose_run(part_source(0))
                gate_up(chunk_codes, by_f_tile, sums)
            if v + RAW_CHUNKS < N_CHUNKS:
                load_chunk(v + RAW_CHUNKS)

            silus = []
            for e in range(2):
                silu_a = silu_pool.tile([P, BANK], F32, tag="silu_a")
                nc.scalar.activation(out=silu_a[:], in_=sums[(e, 0)][:], func=SILU)
                silus.append(silu_a)

            chunk_codes = new_codes()
            quantise(grouped, chunk_codes[0], chunk_codes[1], pieces=2)
            if waiting is not None:
                quantise_h(waiting[0], waiting[1])
                waiting = None

            if v % 2 == 0:
                planes = plane_pool.tile([P, 4, TOKENS], BF16, tag="planes")
            for e in range(2):
                nc.vector.tensor_tensor(
                    out=planes[:, 2 * (v % 2) + e, :], in0=silus[e][:], in1=sums[(e, 1)][:], op=MULT
                )
            if v % 2 == 1:
                grouped_h = h_pool.tile([P, TOKENS, 4], BF16, tag="grouped_h", align_bytes=64)
                nc.vector.tensor_copy(
                    out=grouped_h[:].rearrange("p (n i) t -> p n t i", i=4),
                    in_=planes[:].rearrange("p t (n i) -> p n t i", i=4),
                )
                waiting = (grouped_h, v // 2)

        part_codes = {0: chunk_codes}

        def down_pass(acc, i, g, first, n):
            codes, scales = part_codes[3 * (first // BANK) + g // 2]
            col = BANK * (g % 2) + first % BANK
            nc.tensor.matmul_mx(
                out=acc,
                lhsT=h_codes[:, g, P * i : P * i + P].bitcast(FP8X4),
                lhsT_scale=h_scales[:, g, P * i : P * i + P],
                rhs=codes[:, col : col + n].bitcast(FP8X4),
                rhs_scale=scales[:, col : col + n],
                start=(g == 0),
                stop=(g == N_PASSES_2 - 1),
            )

        tile_sums = None
        for part in range(N_PARTS):
            half, pair = part // 3, part % 3
            n_tiles = 4 if half == 0 else 3
            if part + 1 < N_PARTS:
                grouped = transpose_run(part_source(part + 1), vector_banks=(1, 3))
            if pair == 0:
                tile_sums = []
                for i in range(n_tiles):
                    acc = mx_psum.tile([P, BANK], F32, tag="acc")
                    tile_sums.append(acc)
            if waiting is not None:
                quantise_h(waiting[0], waiting[1])
                waiting = None
            for i in range(n_tiles):
                for g in range(2 * pair, 2 * pair + 2):
                    down_pass(tile_sums[i][:], i, g, BANK * half, BANK)
            if part + 1 < N_PARTS:
                part_codes[part + 1] = new_codes()
                quantise(grouped, part_codes[part + 1][0], part_codes[part + 1][1], pieces=2)
            if pair == 2:
                for i in range(n_tiles):
                    result = out_pool.tile([P, BANK], F32, tag="result")
                    if i % 2 == 0:
                        nc.scalar.copy(out=result[:], in_=tile_sums[i][:])
                    else:
                        nc.vector.tensor_copy(out=result[:], in_=tile_sums[i][:])
                    nc.sync.dma_start(
                        out=out_rows[P * i : P * i + P, BANK * half : BANK * half + BANK], in_=result[:]
                    )

        for q in range(2):
            first = BANK + 256 * q
            t_bank = t_psum.tile([P, 2, 256], F32, tag="t_bank")
            for g in range(N_PASSES_2):
                down_pass(t_bank[:, 0, :], 3, g, first, 256)
            result = tail_pool.tile([P, 256], F32, tag="tail_result")
            if q == 0:
                nc.vector.tensor_copy(out=result[:], in_=t_bank[:, 0, :])
            else:
                nc.scalar.copy(out=result[:], in_=t_bank[:, 0, :])
            nc.sync.dma_start(out=out_rows[3 * P : 4 * P, first : first + 256], in_=result[:])
